import numpy as np
import ml_dtypes


def mxq(x, axis, fmt="e4m3"):
    dtype, down = {"e4m3": (ml_dtypes.float8_e4m3fn, 7), "e5m2": (ml_dtypes.float8_e5m2, 14)}[fmt]
    v = np.moveaxis(np.asarray(x, np.float32).astype(ml_dtypes.bfloat16).astype(np.float64), axis, -1)
    blocks = v.reshape(v.shape[:-1] + (-1, 32))
    amax = np.abs(blocks).max(-1, keepdims=True)
    byte = np.maximum(np.where(amax > 0, np.frexp(amax)[1] - 1 + 127, 0) - down, 1)
    scale = np.exp2(byte - 127.0)
    codes = (blocks / scale).astype(np.float32).astype(dtype).astype(np.float64)
    return np.moveaxis((codes * scale).reshape(v.shape), -1, axis)


WIDE = False


def mx_kscale(k):
    if not WIDE:
        return np.ones(k)
    levels = np.array([10, -10, 5, -5, 0])
    a = np.random.permutation(np.resize(levels, k // 512 * 4)).reshape(k // 512, 4)
    idx = np.arange(k)
    return np.exp2(a[idx // 512, idx % 128 // 32])


BF16 = ml_dtypes.bfloat16


def bf(x):
    return np.asarray(x, np.float32).astype(BF16)


def f64(x):
    return np.asarray(x).astype(np.float64)


E2M1 = np.array([0.0, 0.5, 1.0, 1.5, 2.0, 3.0, 4.0, 6.0, -0.0, -0.5, -1.0, -1.5, -2.0, -3.0, -4.0, -6.0])


def pack_weight(w, fmt):
    k, n = w.shape
    w = f64(bf(w)).reshape(k // 32, 32, n)
    amax = np.abs(w).max(1)
    if fmt == "e4m3":
        byte = np.frexp(amax)[1] - 1 + 127 - 7
    else:
        mant, ex = np.frexp(amax / 6.0)
        byte = np.where(mant > 0.5, ex, ex - 1) + 127
    byte = np.clip(np.where(amax > 0, byte, 1), 1, 254)
    scaled = (w * np.exp2(127.0 - byte)[:, None, :]).reshape(k, n).astype(np.float32)
    by_word = np.ascontiguousarray(scaled.reshape(k // 512, 128, 4, n).transpose(0, 1, 3, 2))
    if fmt == "e4m3":
        words = by_word.astype(ml_dtypes.float8_e4m3fn).view(np.uint8)
    else:
        c = by_word.astype(ml_dtypes.float4_e2m1fn).view(np.uint8) & 0xF
        words = c[..., 0::2] | (c[..., 1::2] << 4)
    return np.ascontiguousarray(words), np.ascontiguousarray(byte.astype(np.uint8).reshape(k // 512, 16, n))


def unpack_weight(words, scales, fmt):
    g, p, n, _ = words.shape
    if fmt == "e4m3":
        vals = np.ascontiguousarray(words).view(ml_dtypes.float8_e4m3fn).astype(np.float64)
    else:
        nib = np.empty((g, p, n, 4), np.uint8)
        nib[..., 0::2] = words & 0xF
        nib[..., 1::2] = words >> 4
        vals = E2M1[nib]
    vals = vals * np.repeat(np.exp2(scales.astype(np.float64) - 127.0), 8, axis=1)[..., None]
    return vals.transpose(0, 1, 3, 2).reshape(g * 512, n)

def pack4(w):
    words, scales = pack_weight(w, "e2m1")
    return words.reshape(words.shape[0], 128, -1), scales


def unpack4(words, scales):
    return unpack_weight(words.reshape(words.shape[0], 128, -1, 2), scales, "e2m1")


B, I, O = 1024, 512, 512
DEGREE = 3
KNOTS = (0.2, 0.4, 0.6, 0.8)
SDIM = DEGREE + 1 + len(KNOTS)
T_MAX = 2.0


def truncated_power_basis(t):
    cols = [np.ones_like(t)]
    for p in range(1, DEGREE + 1):
        cols.append(t ** p)
    for c in KNOTS:
        cols.append(np.maximum(t - c, 0.0) ** DEGREE)
    return np.stack(cols, axis=1)


def setup_inputs():
    s = mx_kscale(I)
    t = np.random.random((B, 1)) * T_MAX
    x = np.random.random((B, I)) * s
    w = np.random.standard_normal((SDIM, I, O)) * (0.52 / np.sqrt(I)) / s[None, :, None]
    words, scales = pack4(w.reshape(-1, O))
    return {"inputs": bf(np.concatenate([t, x], axis=1)), "W_wts_words": words, "W_wts_scales": scales,
            "b_wts": bf(np.random.standard_normal((SDIM, O)) * 0.3)}


def reference(inputs, W_wts_words, W_wts_scales, b_wts):
    inputs = f64(inputs)
    treatment = inputs[:, 0]
    features = inputs[:, 1:]
    basis = truncated_power_basis(treatment)
    Wk = unpack4(W_wts_words, W_wts_scales).reshape(SDIM, I, O)
    P = mxq(features, 1, "e4m3") @ Wk
    out = (basis.T[:, :, None] * P).sum(0)
    out = out + (basis[:, :, None] * f64(b_wts)[None, :, :]).sum(1)
    return out

@@ -1,0 +1,180 @@
+from contextlib import ExitStack
+
+import concourse.mybir as mybir
+from concourse.masks import make_identity
+
+F32 = mybir.dt.float32
+BF16 = mybir.dt.bfloat16
+I32 = mybir.dt.int32
+U8 = mybir.dt.uint8
+U32 = mybir.dt.uint32
+FP8X4 = mybir.dt.float8_e4m3fn_x4
+FP4X4 = mybir.dt.float4_e2m1fn_x4
+ALU = mybir.AluOpType
+ACT = mybir.ActivationFunctionType
+
+P = 128
+PACK = 4
+BATCH, FEATURES, OUTPUTS = 1024, 512, 512
+KNOTS = (0.2, 0.4, 0.6, 0.8)
+TERMS = 4 + len(KNOTS)
+TILES = BATCH // P
+PAIRS = TILES // 2
+WORDS = FEATURES // 2
+PIECES = 4
+QUARTER = P // (PIECES * TERMS)
+
+FLOPS = 2 * BATCH * FEATURES * OUTPUTS * TERMS + 2 * BATCH * TERMS * OUTPUTS
+
+
+def tile_vclinear_e_kernel(tc, inputs, W_wts_words, W_wts_scales, b_wts, out):
+    nc = tc.nc
+    in_rows = inputs.rearrange("(p j) c -> p j c", j=TILES)
+    out_rows = out.rearrange("(p j) o -> p j o", j=TILES)
+
+    with ExitStack() as stack:
+        keep = stack.enter_context(tc.tile_pool(name="keep", bufs=1))
+        work = stack.enter_context(tc.tile_pool(name="work", bufs=4))
+        psum = stack.enter_context(tc.psum_pool(name="psum", bufs=8))
+
+        w_planes = keep.tile([P, TERMS, OUTPUTS], U8, align_bytes=64)
+        nc.vector.memset(w_planes[:].bitcast(I32), 0)
+        bias_rows = keep.tile([P, QUARTER, OUTPUTS], BF16)
+        nc.vector.memset(bias_rows[:].bitcast(I32), 0)
+
+        t_bf = keep.tile([P, TILES, 1], BF16)
+        with nc.allow_non_contiguous_dma(reason="the treatment is one column of inputs"):
+            nc.scalar.dma_start(out=t_bf[:], in_=in_rows[:, :, 0:1])
+        for i in range(QUARTER):
+            nc.scalar.dma_start(
+                out=bias_rows[32 * i : 32 * (i + 1), i, :],
+                in_=b_wts.unsqueeze(0).to_broadcast([PIECES, TERMS, OUTPUTS]),
+            )
+
+        x_sb = keep.tile([P, TILES, FEATURES], BF16)
+        w_words = keep.tile([P, TERMS, 2 * OUTPUTS], U8, align_bytes=64)
+
+        def load_x(q):
+            nc.sync.dma_start(out=x_sb[:, 2 * q : 2 * q + 2, :], in_=in_rows[:, 2 * q : 2 * q + 2, 1:])
+
+        def load_w(first, last):
+            nc.sync.dma_start(
+                out=w_words[:, first:last, :].bitcast(I32),
+                in_=W_wts_words[first:last].rearrange("g p c -> p g c").bitcast(I32),
+            )
+
+        load_x(0)
+        for q in range(8):
+            nc.sync.dma_start(
+                out=w_planes[32 * (q // 4) + q % 4 : P : 64].bitcast(I32),
+                in_=W_wts_scales[:, q : 16 : 8, :].rearrange("g h n -> h g n").bitcast(I32),
+            )
+        load_w(0, 2)
+        load_w(2, 4)
+        load_w(4, 8)
+        for q in range(1, PAIRS):
+            load_x(q)
+
+        ident_f32 = keep.tile([P, P], F32)
+        make_identity(nc, ident_f32[:])
+        ident_bf = keep.tile([P, P], BF16)
+        make_identity(nc, ident_bf[:])
+
+        basis = keep.tile([P, TILES, TERMS], F32)
+        t = basis[:, :, 1:2]
+        nc.vector.memset(basis[:, :, 0:1], 1.0)
+        nc.vector.tensor_copy(out=t, in_=t_bf[:])
+        nc.vector.tensor_mul(out=basis[:, :, 2:3], in0=t, in1=t)
+        nc.vector.tensor_mul(out=basis[:, :, 3:4], in0=basis[:, :, 2:3], in1=t)
+        hinge = keep.tile([P, TILES, len(KNOTS)], F32)
+        for c, knot in enumerate(KNOTS):
+            nc.vector.tensor_scalar(
+                out=hinge[:, :, c : c + 1], in0=t, scalar1=knot, scalar2=0.0, op0=ALU.subtract, op1=ALU.max
+            )
+        hinge_sq = keep.tile([P, TILES, len(KNOTS)], F32)
+        nc.vector.tensor_mul(out=hinge_sq[:], in0=hinge[:], in1=hinge[:])
+        nc.vector.tensor_mul(out=basis[:, :, 4:], in0=hinge_sq[:], in1=hinge[:])
+
+        pieces = keep.tile([P, TILES, PIECES, TERMS], BF16)
+        nc.vector.memset(pieces[:], 0.0)
+        rest = basis
+        for c in range(3):
+            nc.vector.tensor_copy(out=pieces[:, :, c, :], in_=rest[:])
+            if c < 2:
+                smaller = keep.tile([P, TILES, TERMS], F32, name="rest%d" % c)
+                nc.vector.tensor_sub(out=smaller[:], in0=rest[:], in1=pieces[:, :, c, :])
+                rest = smaller
+        pieces_cols = pieces[:].rearrange("p j c s -> p (j c s)")
+        piecesT_ps = psum.tile([P, 2, P], BF16, tag="bank")
+        for h in range(2):
+            nc.tensor.transpose(piecesT_ps[:, h, :], pieces_cols[:, P * h : P * (h + 1)], ident_bf[:])
+        piecesT = keep.tile([P, 2, P], BF16)
+        nc.vector.tensor_copy(out=piecesT[:], in_=piecesT_ps[:])
+
+        x_words = x_sb[:].bitcast(F32)
+        grouped = keep.tile([P, TILES * P * PACK], BF16, align_bytes=64)
+        grouped_words = grouped[:].bitcast(F32).rearrange("p (j b u) -> p j b u", j=TILES, u=2)
+        x_codes = keep.tile([P, TILES * P], U32, align_bytes=64)
+        x_planes = keep.tile([P, TILES * P], U8, align_bytes=64)
+        for q in range(PAIRS):
+            xT = psum.tile([P, 2, 2, P], F32, tag="bank")
+            for i in range(2):
+                for u in range(2):
+                    nc.tensor.transpose(xT[:, i, u, :], x_words[:, 2 * q + i, u:WORDS:2], ident_f32[:])
+            nc.scalar.copy(out=grouped_words[:, 2 * q : 2 * q + 2], in_=xT[:].rearrange("p i u b -> p i b u"))
+            cols = slice(2 * P * q, 2 * P * (q + 1))
+            nc.vector.quantize_mx(
+                out=x_codes[:, cols].bitcast(FP8X4),
+                scales=x_planes[:, cols],
+                in_=grouped[:, 2 * P * PACK * q : 2 * P * PACK * (q + 1)],
+            )
+
+        def product(j, s):
+            bank = psum.tile([P, OUTPUTS], F32, tag="bank", name="bank")
+            nc.tensor.matmul_mx(
+                out=bank[:],
+                lhsT=x_codes[:, P * j : P * (j + 1)].bitcast(FP8X4),
+                lhsT_scale=x_planes[:, P * j : P * (j + 1)],
+                rhs=w_words[:, s, :].bitcast(FP4X4),
+                rhs_scale=w_planes[:, s, :],
+                start=True,
+                stop=True,
+            )
+            return bank
+
+        for q in range(PAIRS):
+            pair = (2 * q, 2 * q + 1)
+            acc = {}
+            side = {}
+            for j in pair:
+                acc[j] = work.tile([P, OUTPUTS], F32, name="acc")
+                nc.scalar.copy(out=acc[j][:], in_=product(j, 0)[:])
+            for j in pair:
+                bias_ps = psum.tile([P, OUTPUTS], F32, tag="bank")
+                nc.tensor.matmul(
+                    out=bias_ps[:],
+                    lhsT=piecesT[:, j // QUARTER, :],
+                    rhs=bias_rows[:, j % QUARTER, :],
+                    start=True,
+                    stop=True,
+                )
+                bias_sb = work.tile([P, OUTPUTS], F32)
+                nc.scalar.copy(out=bias_sb[:], in_=bias_ps[:])
+                linear = work.tile([P, OUTPUTS], F32)
+                nc.scalar.activation(out=linear[:], in_=product(j, 1)[:], func=ACT.Copy, scale=basis[:, j, 1:2])
+                side[j] = work.tile([P, OUTPUTS], F32, name="side")
+                nc.gpsimd.tensor_add(out=side[j][:], in0=bias_sb[:], in1=linear[:])
+            for s in range(2, TERMS):
+                for j in pair:
+                    nc.vector.scalar_tensor_tensor(
+                        out=acc[j][:],
+                        in0=product(j, s)[:],
+                        scalar=basis[:, j, s : s + 1],
+                        in1=acc[j][:],
+                        op0=ALU.mult,
+                        op1=ALU.add,
+                    )
+            for j in pair:
+                result = work.tile([P, OUTPUTS], F32)
+                nc.gpsimd.tensor_add(out=result[:], in0=acc[j][:], in1=side[j][:])
+                nc.sync.dma_start(out=out_rows[:, j, :], in_=result[:])

@@ -22,7 +22,8 @@ TILES = BATCH // P
 PAIRS = TILES // 2
 WORDS = FEATURES // 2
 PIECES = 4
-QUARTER = P // (PIECES * TERMS)
+FIRST_HALF = range(2, 5)
+SECOND_HALF = range(5, TERMS)
 
 FLOPS = 2 * BATCH * FEATURES * OUTPUTS * TERMS + 2 * BATCH * TERMS * OUTPUTS
 
@@ -34,25 +35,20 @@ def tile_vclinear_e_kernel(tc, inputs, W_wts_words, W_wts_scales, b_wts, out):
 
     with ExitStack() as stack:
         keep = stack.enter_context(tc.tile_pool(name="keep", bufs=1))
-        work = stack.enter_context(tc.tile_pool(name="work", bufs=4))
+        work = stack.enter_context(tc.tile_pool(name="work", bufs=6))
         psum = stack.enter_context(tc.psum_pool(name="psum", bufs=8))
+        stack.enter_context(tc.manual_schedule())
 
         w_planes = keep.tile([P, TERMS, OUTPUTS], U8, align_bytes=64)
         nc.vector.memset(w_planes[:].bitcast(I32), 0)
-        bias_rows = keep.tile([P, QUARTER, OUTPUTS], BF16)
+        bias_rows = keep.tile([P, OUTPUTS], BF16)
         nc.vector.memset(bias_rows[:].bitcast(I32), 0)
-
-        t_bf = keep.tile([P, TILES, 1], BF16)
-        with nc.allow_non_contiguous_dma(reason="the treatment is one column of inputs"):
-            nc.scalar.dma_start(out=t_bf[:], in_=in_rows[:, :, 0:1])
-        for i in range(QUARTER):
-            nc.scalar.dma_start(
-                out=bias_rows[32 * i : 32 * (i + 1), i, :],
-                in_=b_wts.unsqueeze(0).to_broadcast([PIECES, TERMS, OUTPUTS]),
-            )
+        pieces = keep.tile([P, TILES, P], BF16)
+        nc.vector.memset(pieces[:].bitcast(I32), 0)
 
         x_sb = keep.tile([P, TILES, FEATURES], BF16)
         w_words = keep.tile([P, TERMS, 2 * OUTPUTS], U8, align_bytes=64)
+        t_bf = keep.tile([P, TILES, 1], BF16)
 
         def load_x(q):
             nc.sync.dma_start(out=x_sb[:, 2 * q : 2 * q + 2, :], in_=in_rows[:, 2 * q : 2 * q + 2, 1:])
@@ -63,22 +59,28 @@ def tile_vclinear_e_kernel(tc, inputs, W_wts_words, W_wts_scales, b_wts, out):
                 in_=W_wts_words[first:last].rearrange("g p c -> p g c").bitcast(I32),
             )
 
+        with nc.allow_non_contiguous_dma(reason="the treatment is one column of inputs"):
+            nc.scalar.dma_start(out=t_bf[:], in_=in_rows[:, :, 0:1])
+        nc.scalar.dma_start(
+            out=bias_rows[0 : PIECES * TERMS, :], in_=b_wts.unsqueeze(0).to_broadcast([PIECES, TERMS, OUTPUTS])
+        )
         load_x(0)
-        for q in range(8):
+        for r in range(4):
             nc.sync.dma_start(
-                out=w_planes[32 * (q // 4) + q % 4 : P : 64].bitcast(I32),
-                in_=W_wts_scales[:, q : 16 : 8, :].rearrange("g h n -> h g n").bitcast(I32),
+                out=w_planes[r:P:32].bitcast(I32),
+                in_=W_wts_scales[:, r:16:4, :].rearrange("g Q n -> Q g n").bitcast(I32),
             )
-        load_w(0, 2)
-        load_w(2, 4)
-        load_w(4, 8)
-        for q in range(1, PAIRS):
-            load_x(q)
+        load_w(0, 1)
+        load_w(1, SECOND_HALF[0])
+        load_x(1)
+        load_w(SECOND_HALF[0], TERMS)
+        load_x(2)
+        load_x(3)
 
         ident_f32 = keep.tile([P, P], F32)
         make_identity(nc, ident_f32[:])
         ident_bf = keep.tile([P, P], BF16)
-        make_identity(nc, ident_bf[:])
+        nc.scalar.copy(out=ident_bf[:], in_=ident_f32[:])
 
         basis = keep.tile([P, TILES, TERMS], F32)
         t = basis[:, :, 1:2]
@@ -95,28 +97,22 @@ def tile_vclinear_e_kernel(tc, inputs, W_wts_words, W_wts_scales, b_wts, out):
         nc.vector.tensor_mul(out=hinge_sq[:], in0=hinge[:], in1=hinge[:])
         nc.vector.tensor_mul(out=basis[:, :, 4:], in0=hinge_sq[:], in1=hinge[:])
 
-        pieces = keep.tile([P, TILES, PIECES, TERMS], BF16)
-        nc.vector.memset(pieces[:], 0.0)
         rest = basis
         for c in range(3):
-            nc.vector.tensor_copy(out=pieces[:, :, c, :], in_=rest[:])
+            piece = pieces[:, :, TERMS * c : TERMS * (c + 1)]
+            nc.vector.tensor_copy(out=piece, in_=rest[:])
             if c < 2:
                 smaller = keep.tile([P, TILES, TERMS], F32, name="rest%d" % c)
-                nc.vector.tensor_sub(out=smaller[:], in0=rest[:], in1=pieces[:, :, c, :])
+                nc.vector.tensor_sub(out=smaller[:], in0=rest[:], in1=piece)
                 rest = smaller
-        pieces_cols = pieces[:].rearrange("p j c s -> p (j c s)")
-        piecesT_ps = psum.tile([P, 2, P], BF16, tag="bank")
-        for h in range(2):
-            nc.tensor.transpose(piecesT_ps[:, h, :], pieces_cols[:, P * h : P * (h + 1)], ident_bf[:])
-        piecesT = keep.tile([P, 2, P], BF16)
-        nc.vector.tensor_copy(out=piecesT[:], in_=piecesT_ps[:])
 
         x_words = x_sb[:].bitcast(F32)
         grouped = keep.tile([P, TILES * P * PACK], BF16, align_bytes=64)
         grouped_words = grouped[:].bitcast(F32).rearrange("p (j b u) -> p j b u", j=TILES, u=2)
         x_codes = keep.tile([P, TILES * P], U32, align_bytes=64)
         x_planes = keep.tile([P, TILES * P], U8, align_bytes=64)
-        for q in range(PAIRS):
+
+        def quantise_pair(q):
             xT = psum.tile([P, 2, 2, P], F32, tag="bank")
             for i in range(2):
                 for u in range(2):
@@ -142,39 +138,54 @@ def tile_vclinear_e_kernel(tc, inputs, W_wts_words, W_wts_scales, b_wts, out):
             )
             return bank
 
-        for q in range(PAIRS):
-            pair = (2 * q, 2 * q + 1)
-            acc = {}
-            side = {}
-            for j in pair:
-                acc[j] = work.tile([P, OUTPUTS], F32, name="acc")
-                nc.scalar.copy(out=acc[j][:], in_=product(j, 0)[:])
-            for j in pair:
-                bias_ps = psum.tile([P, OUTPUTS], F32, tag="bank")
-                nc.tensor.matmul(
-                    out=bias_ps[:],
-                    lhsT=piecesT[:, j // QUARTER, :],
-                    rhs=bias_rows[:, j % QUARTER, :],
-                    start=True,
-                    stop=True,
-                )
-                bias_sb = work.tile([P, OUTPUTS], F32)
-                nc.scalar.copy(out=bias_sb[:], in_=bias_ps[:])
-                linear = work.tile([P, OUTPUTS], F32)
-                nc.scalar.activation(out=linear[:], in_=product(j, 1)[:], func=ACT.Copy, scale=basis[:, j, 1:2])
-                side[j] = work.tile([P, OUTPUTS], F32, name="side")
-                nc.gpsimd.tensor_add(out=side[j][:], in0=bias_sb[:], in1=linear[:])
-            for s in range(2, TERMS):
+        def add_products(total, pair, terms):
+            for s in terms:
                 for j in pair:
                     nc.vector.scalar_tensor_tensor(
-                        out=acc[j][:],
+                        out=total[j][:],
                         in0=product(j, s)[:],
                         scalar=basis[:, j, s : s + 1],
-                        in1=acc[j][:],
+                        in1=total[j][:],
                         op0=ALU.mult,
                         op1=ALU.add,
                     )
-            for j in pair:
-                result = work.tile([P, OUTPUTS], F32)
-                nc.gpsimd.tensor_add(out=result[:], in0=acc[j][:], in1=side[j][:])
-                nc.sync.dma_start(out=out_rows[:, j, :], in_=result[:])
+
+        quantise_pair(0)
+
+        piecesT_ps = psum.tile([P, TILES, P], BF16, tag="bank")
+        for j in range(TILES):
+            nc.tensor.transpose(piecesT_ps[:, j, :], pieces[:, j, :], ident_bf[:])
+        piecesT = keep.tile([P, TILES, P], BF16)
+        nc.scalar.copy(out=piecesT[:], in_=piecesT_ps[:])
+
+        early = {}
+        total = {}
+        for q in range(PAIRS + 1):
+            if q < PAIRS:
+                pair = (2 * q, 2 * q + 1)
+                for j in pair:
+                    early[j] = work.tile([P, OUTPUTS], F32, name="early")
+                    nc.scalar.copy(out=early[j][:], in_=product(j, 0)[:])
+                add_products(early, pair, FIRST_HALF)
+                side = {}
+                for j in pair:
+                    bias_ps = psum.tile([P, OUTPUTS], F32, tag="bank")
+                    nc.tensor.matmul(out=bias_ps[:], lhsT=piecesT[:, j, :], rhs=bias_rows[:], start=True, stop=True)
+                    bias_sb = work.tile([P, OUTPUTS], F32)
+                    nc.scalar.copy(out=bias_sb[:], in_=bias_ps[:])
+                    linear = work.tile([P, OUTPUTS], F32)
+                    nc.scalar.activation(
+                        out=linear[:], in_=product(j, 1)[:], func=ACT.Copy, scale=basis[:, j, 1:2]
+                    )
+                    side[j] = work.tile([P, OUTPUTS], F32, name="side")
+                    nc.gpsimd.tensor_add(out=side[j][:], in0=bias_sb[:], in1=linear[:])
+                for j in pair:
+                    total[j] = work.tile([P, OUTPUTS], F32, name="total")
+                    nc.gpsimd.tensor_add(out=total[j][:], in0=early[j][:], in1=side[j][:])
+            if q > 0:
+                pair = (2 * q - 2, 2 * q - 1)
+                add_products(total, pair, SECOND_HALF)
+                for j in pair:
+                    nc.sync.dma_start(out=out_rows[:, j, :], in_=total[j][:])
+            if q + 1 < PAIRS:
+                quantise_pair(q + 1)

@@ -60,11 +60,9 @@ def tile_vclinear_e_kernel(tc, inputs, W_wts_words, W_wts_scales, b_wts, out):
             )
 
         with nc.allow_non_contiguous_dma(reason="the treatment is one column of inputs"):
-            nc.scalar.dma_start(out=t_bf[:], in_=in_rows[:, :, 0:1])
-        nc.scalar.dma_start(
-            out=bias_rows[0 : PIECES * TERMS, :], in_=b_wts.unsqueeze(0).to_broadcast([PIECES, TERMS, OUTPUTS])
-        )
+            nc.sync.dma_start(out=t_bf[:], in_=in_rows[:, :, 0:1])
         load_x(0)
+        load_x(1)
         for r in range(4):
             nc.sync.dma_start(
                 out=w_planes[r:P:32].bitcast(I32),
@@ -72,7 +70,9 @@ def tile_vclinear_e_kernel(tc, inputs, W_wts_words, W_wts_scales, b_wts, out):
             )
         load_w(0, 1)
         load_w(1, SECOND_HALF[0])
-        load_x(1)
+        nc.sync.dma_start(
+            out=bias_rows[0 : PIECES * TERMS, :], in_=b_wts.unsqueeze(0).to_broadcast([PIECES, TERMS, OUTPUTS])
+        )
         load_w(SECOND_HALF[0], TERMS)
         load_x(2)
         load_x(3)
@@ -83,28 +83,38 @@ def tile_vclinear_e_kernel(tc, inputs, W_wts_words, W_wts_scales, b_wts, out):
         nc.scalar.copy(out=ident_bf[:], in_=ident_f32[:])
 
         basis = keep.tile([P, TILES, TERMS], F32)
-        t = basis[:, :, 1:2]
-        nc.vector.memset(basis[:, :, 0:1], 1.0)
-        nc.vector.tensor_copy(out=t, in_=t_bf[:])
-        nc.vector.tensor_mul(out=basis[:, :, 2:3], in0=t, in1=t)
-        nc.vector.tensor_mul(out=basis[:, :, 3:4], in0=basis[:, :, 2:3], in1=t)
         hinge = keep.tile([P, TILES, len(KNOTS)], F32)
-        for c, knot in enumerate(KNOTS):
-            nc.vector.tensor_scalar(
-                out=hinge[:, :, c : c + 1], in0=t, scalar1=knot, scalar2=0.0, op0=ALU.subtract, op1=ALU.max
-            )
         hinge_sq = keep.tile([P, TILES, len(KNOTS)], F32)
-        nc.vector.tensor_mul(out=hinge_sq[:], in0=hinge[:], in1=hinge[:])
-        nc.vector.tensor_mul(out=basis[:, :, 4:], in0=hinge_sq[:], in1=hinge[:])
+        piecesT = keep.tile([P, TILES, P], BF16)
 
-        rest = basis
-        for c in range(3):
-            piece = pieces[:, :, TERMS * c : TERMS * (c + 1)]
-            nc.vector.tensor_copy(out=piece, in_=rest[:])
-            if c < 2:
-                smaller = keep.tile([P, TILES, TERMS], F32, name="rest%d" % c)
-                nc.vector.tensor_sub(out=smaller[:], in0=rest[:], in1=piece)
-                rest = smaller
+        def make_basis():
+            t = basis[:, :, 1:2]
+            nc.vector.memset(basis[:, :, 0:1], 1.0)
+            nc.vector.tensor_copy(out=t, in_=t_bf[:])
+            nc.vector.tensor_mul(out=basis[:, :, 2:3], in0=t, in1=t)
+            nc.vector.tensor_mul(out=basis[:, :, 3:4], in0=basis[:, :, 2:3], in1=t)
+            for c, knot in enumerate(KNOTS):
+                nc.vector.tensor_scalar(
+                    out=hinge[:, :, c : c + 1], in0=t, scalar1=knot, scalar2=0.0, op0=ALU.subtract, op1=ALU.max
+                )
+            nc.vector.tensor_mul(out=hinge_sq[:], in0=hinge[:], in1=hinge[:])
+            nc.vector.tensor_mul(out=basis[:, :, 4:], in0=hinge_sq[:], in1=hinge[:])
+
+        def split_basis():
+            rest = basis
+            for c in range(3):
+                piece = pieces[:, :, TERMS * c : TERMS * (c + 1)]
+                nc.vector.tensor_copy(out=piece, in_=rest[:])
+                if c < 2:
+                    smaller = keep.tile([P, TILES, TERMS], F32, name="rest%d" % c)
+                    nc.vector.tensor_sub(out=smaller[:], in0=rest[:], in1=piece)
+                    rest = smaller
+
+        def transpose_pieces():
+            piecesT_ps = psum.tile([P, TILES, P], BF16, tag="bank")
+            for j in range(TILES):
+                nc.tensor.transpose(piecesT_ps[:, j, :], pieces[:, j, :], ident_bf[:])
+            nc.vector.tensor_copy(out=piecesT[:], in_=piecesT_ps[:])
 
         x_words = x_sb[:].bitcast(F32)
         grouped = keep.tile([P, TILES * P * PACK], BF16, align_bytes=64)
@@ -138,54 +148,57 @@ def tile_vclinear_e_kernel(tc, inputs, W_wts_words, W_wts_scales, b_wts, out):
             )
             return bank
 
-        def add_products(total, pair, terms):
+        def add_products(sums, pair, terms):
             for s in terms:
                 for j in pair:
                     nc.vector.scalar_tensor_tensor(
-                        out=total[j][:],
+                        out=sums[j][:],
                         in0=product(j, s)[:],
                         scalar=basis[:, j, s : s + 1],
-                        in1=total[j][:],
+                        in1=sums[j][:],
                         op0=ALU.mult,
                         op1=ALU.add,
                     )
 
-        quantise_pair(0)
+        def first_half(q):
+            pair = (2 * q, 2 * q + 1)
+            early = {}
+            side = {}
+            for j in pair:
+                early[j] = work.tile([P, OUTPUTS], F32, name="early")
+                nc.scalar.copy(out=early[j][:], in_=product(j, 0)[:])
+            add_products(early, pair, FIRST_HALF[:1])
+            for j in pair:
+                bias_ps = psum.tile([P, OUTPUTS], F32, tag="bank")
+                nc.tensor.matmul(out=bias_ps[:], lhsT=piecesT[:, j, :], rhs=bias_rows[:], start=True, stop=True)
+                bias_sb = work.tile([P, OUTPUTS], F32)
+                nc.scalar.copy(out=bias_sb[:], in_=bias_ps[:])
+                linear = work.tile([P, OUTPUTS], F32)
+                nc.scalar.activation(out=linear[:], in_=product(j, 1)[:], func=ACT.Copy, scale=basis[:, j, 1:2])
+                side[j] = work.tile([P, OUTPUTS], F32, name="side")
+                nc.gpsimd.tensor_add(out=side[j][:], in0=bias_sb[:], in1=linear[:])
+            add_products(early, pair, FIRST_HALF[1:])
+            for j in pair:
+                total[j] = work.tile([P, OUTPUTS], F32, name="total")
+                nc.gpsimd.tensor_add(out=total[j][:], in0=early[j][:], in1=side[j][:])
 
-        piecesT_ps = psum.tile([P, TILES, P], BF16, tag="bank")
-        for j in range(TILES):
-            nc.tensor.transpose(piecesT_ps[:, j, :], pieces[:, j, :], ident_bf[:])
-        piecesT = keep.tile([P, TILES, P], BF16)
-        nc.scalar.copy(out=piecesT[:], in_=piecesT_ps[:])
+        def second_half(q):
+            pair = (2 * q, 2 * q + 1)
+            add_products(total, pair, SECOND_HALF)
+            for j in pair:
+                nc.sync.dma_start(out=out_rows[:, j, :], in_=total[j][:])
 
-        early = {}
         total = {}
-        for q in range(PAIRS + 1):
-            if q < PAIRS:
-                pair = (2 * q, 2 * q + 1)
-                for j in pair:
-                    early[j] = work.tile([P, OUTPUTS], F32, name="early")
-                    nc.scalar.copy(out=early[j][:], in_=product(j, 0)[:])
-                add_products(early, pair, FIRST_HALF)
-                side = {}
-                for j in pair:
-                    bias_ps = psum.tile([P, OUTPUTS], F32, tag="bank")
-                    nc.tensor.matmul(out=bias_ps[:], lhsT=piecesT[:, j, :], rhs=bias_rows[:], start=True, stop=True)
-                    bias_sb = work.tile([P, OUTPUTS], F32)
-                    nc.scalar.copy(out=bias_sb[:], in_=bias_ps[:])
-                    linear = work.tile([P, OUTPUTS], F32)
-                    nc.scalar.activation(
-                        out=linear[:], in_=product(j, 1)[:], func=ACT.Copy, scale=basis[:, j, 1:2]
-                    )
-                    side[j] = work.tile([P, OUTPUTS], F32, name="side")
-                    nc.gpsimd.tensor_add(out=side[j][:], in0=bias_sb[:], in1=linear[:])
-                for j in pair:
-                    total[j] = work.tile([P, OUTPUTS], F32, name="total")
-                    nc.gpsimd.tensor_add(out=total[j][:], in0=early[j][:], in1=side[j][:])
-            if q > 0:
-                pair = (2 * q - 2, 2 * q - 1)
-                add_products(total, pair, SECOND_HALF)
-                for j in pair:
-                    nc.sync.dma_start(out=out_rows[:, j, :], in_=total[j][:])
+
+        make_basis()
+        split_basis()
+        quantise_pair(0)
+        quantise_pair(1)
+        transpose_pieces()
+        first_half(0)
+        for q in range(1, PAIRS):
+            first_half(q)
             if q + 1 < PAIRS:
                 quantise_pair(q + 1)
+            second_half(q - 1)
+        second_half(PAIRS - 1)

@@ -19,11 +19,11 @@ BATCH, FEATURES, OUTPUTS = 1024, 512, 512
 KNOTS = (0.2, 0.4, 0.6, 0.8)
 TERMS = 4 + len(KNOTS)
 TILES = BATCH // P
-PAIRS = TILES // 2
 WORDS = FEATURES // 2
 PIECES = 4
-FIRST_HALF = range(2, 5)
-SECOND_HALF = range(5, TERMS)
+GROUP = P // (PIECES * TERMS)
+CHAIN = (1, 2, 3, 4, 5, 6)
+SCALED = 7
 
 FLOPS = 2 * BATCH * FEATURES * OUTPUTS * TERMS + 2 * BATCH * TERMS * OUTPUTS
 
@@ -35,16 +35,17 @@ def tile_vclinear_e_kernel(tc, inputs, W_wts_words, W_wts_scales, b_wts, out):
 
     with ExitStack() as stack:
         keep = stack.enter_context(tc.tile_pool(name="keep", bufs=1))
-        work = stack.enter_context(tc.tile_pool(name="work", bufs=6))
         psum = stack.enter_context(tc.psum_pool(name="psum", bufs=8))
         stack.enter_context(tc.manual_schedule())
 
         w_planes = keep.tile([P, TERMS, OUTPUTS], U8, align_bytes=64)
         nc.vector.memset(w_planes[:].bitcast(I32), 0)
-        bias_rows = keep.tile([P, OUTPUTS], BF16)
-        nc.vector.memset(bias_rows[:].bitcast(I32), 0)
-        pieces = keep.tile([P, TILES, P], BF16)
+        pieces = keep.tile([P, TILES, PIECES * TERMS], BF16)
         nc.vector.memset(pieces[:].bitcast(I32), 0)
+        bias_rhs = keep.tile([P, GROUP, OUTPUTS], BF16)
+        nc.vector.memset(bias_rhs[:].bitcast(I32), 0)
+        basis = keep.tile([P, TILES, TERMS], F32)
+        nc.vector.memset(basis[:, :, 0:1], 1.0)
 
         x_sb = keep.tile([P, TILES, FEATURES], BF16)
         w_words = keep.tile([P, TERMS, 2 * OUTPUTS], U8, align_bytes=64)
@@ -62,18 +63,21 @@ def tile_vclinear_e_kernel(tc, inputs, W_wts_words, W_wts_scales, b_wts, out):
         with nc.allow_non_contiguous_dma(reason="the treatment is one column of inputs"):
             nc.sync.dma_start(out=t_bf[:], in_=in_rows[:, :, 0:1])
         load_x(0)
-        load_x(1)
         for r in range(4):
             nc.sync.dma_start(
                 out=w_planes[r:P:32].bitcast(I32),
                 in_=W_wts_scales[:, r:16:4, :].rearrange("g Q n -> Q g n").bitcast(I32),
             )
-        load_w(0, 1)
-        load_w(1, SECOND_HALF[0])
-        nc.sync.dma_start(
-            out=bias_rows[0 : PIECES * TERMS, :], in_=b_wts.unsqueeze(0).to_broadcast([PIECES, TERMS, OUTPUTS])
-        )
-        load_w(SECOND_HALF[0], TERMS)
+        load_w(0, 2)
+        load_w(2, 5)
+        load_w(5, TERMS)
+        load_x(1)
+        rows = PIECES * TERMS
+        for a in range(GROUP):
+            nc.sync.dma_start(
+                out=bias_rhs[rows * a : rows * (a + 1), a, :],
+                in_=b_wts.unsqueeze(0).to_broadcast([PIECES, TERMS, OUTPUTS]),
+            )
         load_x(2)
         load_x(3)
 
@@ -82,39 +86,37 @@ def tile_vclinear_e_kernel(tc, inputs, W_wts_words, W_wts_scales, b_wts, out):
         ident_bf = keep.tile([P, P], BF16)
         nc.scalar.copy(out=ident_bf[:], in_=ident_f32[:])
 
-        basis = keep.tile([P, TILES, TERMS], F32)
         hinge = keep.tile([P, TILES, len(KNOTS)], F32)
         hinge_sq = keep.tile([P, TILES, len(KNOTS)], F32)
-        piecesT = keep.tile([P, TILES, P], BF16)
+        nc.vector.tensor_copy(out=basis[:, :, 1:2], in_=t_bf[:])
+        for c, knot in enumerate(KNOTS):
+            nc.vector.tensor_scalar(
+                out=hinge[:, :, c : c + 1], in0=t_bf[:], scalar1=knot, scalar2=0.0, op0=ALU.subtract, op1=ALU.max
+            )
+        nc.vector.tensor_mul(out=basis[:, :, 2:3], in0=t_bf[:], in1=t_bf[:])
+        nc.vector.tensor_mul(out=hinge_sq[:], in0=hinge[:], in1=hinge[:])
+        nc.vector.tensor_mul(out=basis[:, :, 3:4], in0=basis[:, :, 2:3], in1=basis[:, :, 1:2])
+        nc.vector.tensor_mul(out=basis[:, :, 4:], in0=hinge_sq[:], in1=hinge[:])
 
-        def make_basis():
-            t = basis[:, :, 1:2]
-            nc.vector.memset(basis[:, :, 0:1], 1.0)
-            nc.vector.tensor_copy(out=t, in_=t_bf[:])
-            nc.vector.tensor_mul(out=basis[:, :, 2:3], in0=t, in1=t)
-            nc.vector.tensor_mul(out=basis[:, :, 3:4], in0=basis[:, :, 2:3], in1=t)
-            for c, knot in enumerate(KNOTS):
-                nc.vector.tensor_scalar(
-                    out=hinge[:, :, c : c + 1], in0=t, scalar1=knot, scalar2=0.0, op0=ALU.subtract, op1=ALU.max
-                )
-            nc.vector.tensor_mul(out=hinge_sq[:], in0=hinge[:], in1=hinge[:])
-            nc.vector.tensor_mul(out=basis[:, :, 4:], in0=hinge_sq[:], in1=hinge[:])
-
-        def split_basis():
-            rest = basis
-            for c in range(3):
-                piece = pieces[:, :, TERMS * c : TERMS * (c + 1)]
-                nc.vector.tensor_copy(out=piece, in_=rest[:])
-                if c < 2:
-                    smaller = keep.tile([P, TILES, TERMS], F32, name="rest%d" % c)
-                    nc.vector.tensor_sub(out=smaller[:], in0=rest[:], in1=piece)
-                    rest = smaller
+        rest = basis
+        for c in range(3):
+            piece = pieces[:, :, TERMS * c : TERMS * (c + 1)]
+            nc.gpsimd.tensor_copy(out=piece, in_=rest[:])
+            if c < 2:
+                smaller = keep.tile([P, TILES, TERMS], F32, name="rest%d" % c)
+                nc.gpsimd.tensor_sub(out=smaller[:], in0=rest[:], in1=piece)
+                rest = smaller
+        piecesT = keep.tile([P, TILES // GROUP, P], BF16)
 
         def transpose_pieces():
-            piecesT_ps = psum.tile([P, TILES, P], BF16, tag="bank")
-            for j in range(TILES):
-                nc.tensor.transpose(piecesT_ps[:, j, :], pieces[:, j, :], ident_bf[:])
-            nc.vector.tensor_copy(out=piecesT[:], in_=piecesT_ps[:])
+            piecesT_ps = psum.tile([P, TILES // GROUP, P], BF16, tag="bank")
+            for h in range(TILES // GROUP):
+                nc.tensor.transpose(
+                    piecesT_ps[:, h, :],
+                    pieces[:, GROUP * h : GROUP * (h + 1), :].rearrange("p j k -> p (j k)"),
+                    ident_bf[:],
+                )
+            nc.scalar.copy(out=piecesT[:], in_=piecesT_ps[:])
 
         x_words = x_sb[:].bitcast(F32)
         grouped = keep.tile([P, TILES * P * PACK], BF16, align_bytes=64)
@@ -122,17 +124,21 @@ def tile_vclinear_e_kernel(tc, inputs, W_wts_words, W_wts_scales, b_wts, out):
         x_codes = keep.tile([P, TILES * P], U32, align_bytes=64)
         x_planes = keep.tile([P, TILES * P], U8, align_bytes=64)
 
-        def quantise_pair(q):
-            xT = psum.tile([P, 2, 2, P], F32, tag="bank")
-            for i in range(2):
+        def turn(first, count):
+            xT = psum.tile([P, count, 2, P], F32, tag="bank", name="xT")
+            for i in range(count):
                 for u in range(2):
-                    nc.tensor.transpose(xT[:, i, u, :], x_words[:, 2 * q + i, u:WORDS:2], ident_f32[:])
-            nc.scalar.copy(out=grouped_words[:, 2 * q : 2 * q + 2], in_=xT[:].rearrange("p i u b -> p i b u"))
-            cols = slice(2 * P * q, 2 * P * (q + 1))
+                    nc.tensor.transpose(xT[:, i, u, :], x_words[:, first + i, u:WORDS:2], ident_f32[:])
+            nc.scalar.copy(
+                out=grouped_words[:, first : first + count], in_=xT[:].rearrange("p i u b -> p i b u")
+            )
+
+        def quantise(first, count):
+            cols = slice(P * first, P * (first + count))
             nc.vector.quantize_mx(
                 out=x_codes[:, cols].bitcast(FP8X4),
                 scales=x_planes[:, cols],
-                in_=grouped[:, 2 * P * PACK * q : 2 * P * PACK * (q + 1)],
+                in_=grouped[:, P * PACK * first : P * PACK * (first + count)],
             )
 
         def product(j, s):
@@ -148,57 +154,130 @@ def tile_vclinear_e_kernel(tc, inputs, W_wts_words, W_wts_scales, b_wts, out):
             )
             return bank
 
-        def add_products(sums, pair, terms):
-            for s in terms:
-                for j in pair:
-                    nc.vector.scalar_tensor_tensor(
-                        out=sums[j][:],
-                        in0=product(j, s)[:],
-                        scalar=basis[:, j, s : s + 1],
-                        in1=sums[j][:],
-                        op0=ALU.mult,
-                        op1=ALU.add,
-                    )
+        acc = {}
+        lin = {}
+        bias_sb = {}
+        side = {}
 
-        def first_half(q):
-            pair = (2 * q, 2 * q + 1)
-            early = {}
-            side = {}
-            for j in pair:
-                early[j] = work.tile([P, OUTPUTS], F32, name="early")
-                nc.scalar.copy(out=early[j][:], in_=product(j, 0)[:])
-            add_products(early, pair, FIRST_HALF[:1])
-            for j in pair:
-                bias_ps = psum.tile([P, OUTPUTS], F32, tag="bank")
-                nc.tensor.matmul(out=bias_ps[:], lhsT=piecesT[:, j, :], rhs=bias_rows[:], start=True, stop=True)
-                bias_sb = work.tile([P, OUTPUTS], F32)
-                nc.scalar.copy(out=bias_sb[:], in_=bias_ps[:])
-                linear = work.tile([P, OUTPUTS], F32)
-                nc.scalar.activation(out=linear[:], in_=product(j, 1)[:], func=ACT.Copy, scale=basis[:, j, 1:2])
-                side[j] = work.tile([P, OUTPUTS], F32, name="side")
-                nc.gpsimd.tensor_add(out=side[j][:], in0=bias_sb[:], in1=linear[:])
-            add_products(early, pair, FIRST_HALF[1:])
-            for j in pair:
-                total[j] = work.tile([P, OUTPUTS], F32, name="total")
-                nc.gpsimd.tensor_add(out=total[j][:], in0=early[j][:], in1=side[j][:])
+        def start_sum(j):
+            acc[j] = keep.tile([P, OUTPUTS], F32, name="acc%d" % j)
+            nc.scalar.copy(out=acc[j][:], in_=product(j, 0)[:])
 
-        def second_half(q):
-            pair = (2 * q, 2 * q + 1)
-            add_products(total, pair, SECOND_HALF)
+        def add_product(j, s):
+            nc.vector.scalar_tensor_tensor(
+                out=acc[j][:],
+                in0=product(j, s)[:],
+                scalar=basis[:, j, s : s + 1],
+                in1=acc[j][:],
+                op0=ALU.mult,
+                op1=ALU.add,
+            )
+
+        def scaled(j):
+            lin[j] = keep.tile([P, OUTPUTS], F32, name="lin%d" % j)
+            nc.scalar.activation(
+                out=lin[j][:], in_=product(j, SCALED)[:], func=ACT.Copy, scale=basis[:, j, SCALED : SCALED + 1]
+            )
+
+        def bias_term(j):
+            bias_ps = psum.tile([P, OUTPUTS], F32, tag="bank")
+            nc.tensor.matmul(
+                out=bias_ps[:], lhsT=piecesT[:, j // GROUP, :], rhs=bias_rhs[:, j % GROUP, :], start=True, stop=True
+            )
+            bias_sb[j] = keep.tile([P, OUTPUTS], F32, name="bias_sb%d" % j)
+            nc.scalar.copy(out=bias_sb[j][:], in_=bias_ps[:])
+
+        def add_side(j):
+            side[j] = keep.tile([P, OUTPUTS], F32, name="side%d" % j)
+            nc.gpsimd.tensor_add(out=side[j][:], in0=bias_sb[j][:], in1=lin[j][:])
+
+        def merge(j):
+            total = keep.tile([P, OUTPUTS], F32, name="total%d" % j)
+            nc.gpsimd.tensor_add(out=total[:], in0=acc[j][:], in1=side[j][:])
+            acc[j] = total
+
+        def store(j):
+            nc.sync.dma_start(out=out_rows[:, j, :], in_=acc[j][:])
+
+        def both(pair, s):
             for j in pair:
-                nc.sync.dma_start(out=out_rows[:, j, :], in_=total[j][:])
+                add_product(j, s)
 
-        total = {}
-
-        make_basis()
-        split_basis()
-        quantise_pair(0)
-        quantise_pair(1)
+        turn(0, 1)
+        quantise(0, 1)
+        turn(1, 1)
+        quantise(1, 1)
+        start_sum(0)
+        add_product(0, 1)
+        start_sum(1)
+        add_product(1, 1)
+        both((0, 1), 2)
+        turn(2, 2)
         transpose_pieces()
-        first_half(0)
-        for q in range(1, PAIRS):
-            first_half(q)
-            if q + 1 < PAIRS:
-                quantise_pair(q + 1)
-            second_half(q - 1)
-        second_half(PAIRS - 1)
+        both((0, 1), 3)
+        quantise(2, 2)
+        scaled(0)
+        scaled(1)
+        both((0, 1), 4)
+        bias_term(0)
+        add_side(0)
+        bias_term(1)
+        add_side(1)
+        both((0, 1), 5)
+        start_sum(2)
+        start_sum(3)
+        both((0, 1), 6)
+        for j in (0, 1):
+            merge(j)
+            store(j)
+        turn(4, 2)
+        both((2, 3), 1)
+        quantise(4, 2)
+        bias_term(2)
+        scaled(2)
+        add_side(2)
+        both((2, 3), 2)
+        bias_term(3)
+        scaled(3)
+        add_side(3)
+        both((2, 3), 3)
+        turn(6, 2)
+        both((2, 3), 4)
+        quantise(6, 2)
+        bias_term(4)
+        scaled(4)
+        add_side(4)
+        both((2, 3), 5)
+        start_sum(4)
+        start_sum(5)
+        both((2, 3), 6)
+        bias_term(5)
+        scaled(5)
+        add_side(5)
+        for j in (2, 3):
+            merge(j)
+            store(j)
+        both((4, 5), 1)
+        start_sum(6)
+        both((4, 5), 2)
+        start_sum(7)
+        both((4, 5), 3)
+        for j in (4, 5):
+            merge(j)
+        bias_term(6)
+        scaled(6)
+        add_side(6)
+        both((6, 7), 1)
+        bias_term(7)
+        both((6, 7), 2)
+        scaled(7)
+        add_side(7)
+        for s in (3, 4, 5, 6):
+            both((6, 7), s)
+        for j in (6, 7):
+            merge(j)
+            store(j)
+        for s in (4, 5, 6):
+            both((4, 5), s)
+        for j in (4, 5):
+            store(j)

@@ -69,9 +69,9 @@ def tile_vclinear_e_kernel(tc, inputs, W_wts_words, W_wts_scales, b_wts, out):
                 in_=W_wts_scales[:, r:16:4, :].rearrange("g Q n -> Q g n").bitcast(I32),
             )
         load_w(0, 2)
+        load_x(1)
         load_w(2, 5)
         load_w(5, TERMS)
-        load_x(1)
         rows = PIECES * TERMS
         for a in range(GROUP):
             nc.sync.dma_start(
@@ -211,28 +211,29 @@ def tile_vclinear_e_kernel(tc, inputs, W_wts_words, W_wts_scales, b_wts, out):
         add_product(0, 1)
         start_sum(1)
         add_product(1, 1)
-        both((0, 1), 2)
         turn(2, 2)
         transpose_pieces()
-        both((0, 1), 3)
+        both((0, 1), 2)
         quantise(2, 2)
         scaled(0)
         scaled(1)
-        both((0, 1), 4)
+        both((0, 1), 3)
         bias_term(0)
         add_side(0)
         bias_term(1)
         add_side(1)
+        both((0, 1), 4)
+        turn(4, 2)
+        turn(6, 2)
         both((0, 1), 5)
+        quantise(4, 4)
         start_sum(2)
         start_sum(3)
         both((0, 1), 6)
         for j in (0, 1):
             merge(j)
             store(j)
-        turn(4, 2)
         both((2, 3), 1)
-        quantise(4, 2)
         bias_term(2)
         scaled(2)
         add_side(2)
@@ -241,9 +242,7 @@ def tile_vclinear_e_kernel(tc, inputs, W_wts_words, W_wts_scales, b_wts, out):
         scaled(3)
         add_side(3)
         both((2, 3), 3)
-        turn(6, 2)
         both((2, 3), 4)
-        quantise(6, 2)
         bias_term(4)
         scaled(4)
         add_side(4)

@@ -24,6 +24,8 @@ PIECES = 4
 GROUP = P // (PIECES * TERMS)
 CHAIN = (1, 2, 3, 4, 5, 6)
 SCALED = 7
+WARM_FIRST = 4
+WARM_SECOND = 3
 
 FLOPS = 2 * BATCH * FEATURES * OUTPUTS * TERMS + 2 * BATCH * TERMS * OUTPUTS
 
@@ -37,6 +39,14 @@ def tile_vclinear_e_kernel(tc, inputs, W_wts_words, W_wts_scales, b_wts, out):
         keep = stack.enter_context(tc.tile_pool(name="keep", bufs=1))
         psum = stack.enter_context(tc.psum_pool(name="psum", bufs=8))
         stack.enter_context(tc.manual_schedule())
+
+        warm = keep.tile([P, OUTPUTS], BF16)
+        nc.gpsimd.memset(warm[:], 0.0)
+        warm_ps = psum.tile([P, OUTPUTS], F32, tag="bank")
+
+        def warm_up(count):
+            for i in range(count):
+                nc.tensor.matmul(out=warm_ps[:], lhsT=warm[:, 0:P], rhs=warm[:], start=True, stop=True)
 
         w_planes = keep.tile([P, TERMS, OUTPUTS], U8, align_bytes=64)
         nc.vector.memset(w_planes[:].bitcast(I32), 0)
@@ -203,10 +213,12 @@ def tile_vclinear_e_kernel(tc, inputs, W_wts_words, W_wts_scales, b_wts, out):
             for j in pair:
                 add_product(j, s)
 
+        warm_up(WARM_FIRST)
         turn(0, 1)
         quantise(0, 1)
         turn(1, 1)
         quantise(1, 1)
+        warm_up(WARM_SECOND)
         start_sum(0)
         add_product(0, 1)
         start_sum(1)

@@ -164,29 +164,36 @@ def tile_vclinear_e_kernel(tc, inputs, W_wts_words, W_wts_scales, b_wts, out):
             )
             return bank
 
-        acc = {}
-        lin = {}
-        bias_sb = {}
-        side = {}
+        def pair_tiles(name):
+            return [keep.tile([P, 2, OUTPUTS], F32, name="%s%d" % (name, q)) for q in range(TILES // 2)]
+
+        acc = pair_tiles("acc")
+        lin = pair_tiles("lin")
+        bias_sb = pair_tiles("bias_sb")
+        side = pair_tiles("side")
+        total = pair_tiles("total")
+        summed = {}
+
+        def half(tiles, j):
+            return tiles[j // 2][:, j % 2, :]
 
         def start_sum(j):
-            acc[j] = keep.tile([P, OUTPUTS], F32, name="acc%d" % j)
-            nc.scalar.copy(out=acc[j][:], in_=product(j, 0)[:])
+            summed[j] = acc
+            nc.scalar.copy(out=half(acc, j), in_=product(j, 0)[:])
 
         def add_product(j, s):
             nc.vector.scalar_tensor_tensor(
-                out=acc[j][:],
+                out=half(summed[j], j),
                 in0=product(j, s)[:],
                 scalar=basis[:, j, s : s + 1],
-                in1=acc[j][:],
+                in1=half(summed[j], j),
                 op0=ALU.mult,
                 op1=ALU.add,
             )
 
         def scaled(j):
-            lin[j] = keep.tile([P, OUTPUTS], F32, name="lin%d" % j)
             nc.scalar.activation(
-                out=lin[j][:], in_=product(j, SCALED)[:], func=ACT.Copy, scale=basis[:, j, SCALED : SCALED + 1]
+                out=half(lin, j), in_=product(j, SCALED)[:], func=ACT.Copy, scale=basis[:, j, SCALED : SCALED + 1]
             )
 
         def bias_term(j):
@@ -194,23 +201,28 @@ def tile_vclinear_e_kernel(tc, inputs, W_wts_words, W_wts_scales, b_wts, out):
             nc.tensor.matmul(
                 out=bias_ps[:], lhsT=piecesT[:, j // GROUP, :], rhs=bias_rhs[:, j % GROUP, :], start=True, stop=True
             )
-            bias_sb[j] = keep.tile([P, OUTPUTS], F32, name="bias_sb%d" % j)
-            nc.scalar.copy(out=bias_sb[j][:], in_=bias_ps[:])
+            nc.scalar.copy(out=half(bias_sb, j), in_=bias_ps[:])
 
-        def add_side(j):
-            side[j] = keep.tile([P, OUTPUTS], F32, name="side%d" % j)
-            nc.gpsimd.tensor_add(out=side[j][:], in0=bias_sb[j][:], in1=lin[j][:])
+        def add_side(q):
+            nc.gpsimd.tensor_add(out=side[q][:], in0=bias_sb[q][:], in1=lin[q][:])
 
-        def merge(j):
-            total = keep.tile([P, OUTPUTS], F32, name="total%d" % j)
-            nc.gpsimd.tensor_add(out=total[:], in0=acc[j][:], in1=side[j][:])
-            acc[j] = total
+        def merge(q):
+            nc.gpsimd.tensor_add(out=total[q][:], in0=acc[q][:], in1=side[q][:])
+            summed[2 * q] = total
+            summed[2 * q + 1] = total
+
+        def merge_one(j):
+            nc.gpsimd.tensor_add(out=half(total, j), in0=half(acc, j), in1=half(side, j))
+            summed[j] = total
 
         def store(j):
-            nc.sync.dma_start(out=out_rows[:, j, :], in_=acc[j][:])
+            nc.sync.dma_start(out=out_rows[:, j, :], in_=half(summed[j], j))
 
-        def both(pair, s):
-            for j in pair:
+        def store_pair(q):
+            nc.sync.dma_start(out=out_rows[:, 2 * q : 2 * q + 2, :], in_=total[q][:])
+
+        def both(q, s):
+            for j in (2 * q, 2 * q + 1):
                 add_product(j, s)
 
         warm_up(WARM_FIRST)
@@ -225,70 +237,63 @@ def tile_vclinear_e_kernel(tc, inputs, W_wts_words, W_wts_scales, b_wts, out):
         add_product(1, 1)
         turn(2, 2)
         transpose_pieces()
-        both((0, 1), 2)
+        both(0, 2)
         quantise(2, 2)
         scaled(0)
         scaled(1)
-        both((0, 1), 3)
+        both(0, 3)
         bias_term(0)
-        add_side(0)
         bias_term(1)
-        add_side(1)
-        both((0, 1), 4)
+        add_side(0)
+        both(0, 4)
         turn(4, 2)
         turn(6, 2)
-        both((0, 1), 5)
+        both(0, 5)
         quantise(4, 4)
         start_sum(2)
         start_sum(3)
-        both((0, 1), 6)
-        for j in (0, 1):
-            merge(j)
-            store(j)
-        both((2, 3), 1)
+        both(0, 6)
+        merge(0)
+        store_pair(0)
+        both(1, 1)
         bias_term(2)
         scaled(2)
-        add_side(2)
-        both((2, 3), 2)
+        both(1, 2)
         bias_term(3)
         scaled(3)
-        add_side(3)
-        both((2, 3), 3)
-        both((2, 3), 4)
+        add_side(1)
+        both(1, 3)
+        both(1, 4)
         bias_term(4)
         scaled(4)
-        add_side(4)
-        both((2, 3), 5)
+        both(1, 5)
         start_sum(4)
         start_sum(5)
-        both((2, 3), 6)
+        both(1, 6)
         bias_term(5)
         scaled(5)
-        add_side(5)
-        for j in (2, 3):
-            merge(j)
-            store(j)
-        both((4, 5), 1)
+        add_side(2)
+        merge(1)
+        store_pair(1)
+        both(2, 1)
         start_sum(6)
-        both((4, 5), 2)
+        both(2, 2)
         start_sum(7)
-        both((4, 5), 3)
-        for j in (4, 5):
-            merge(j)
+        both(2, 3)
+        merge(2)
         bias_term(6)
         scaled(6)
-        add_side(6)
-        both((6, 7), 1)
+        both(3, 1)
         bias_term(7)
-        both((6, 7), 2)
+        both(3, 2)
         scaled(7)
-        add_side(7)
+        add_side(3)
         for s in (3, 4, 5, 6):
-            both((6, 7), s)
+            both(3, s)
         for j in (6, 7):
-            merge(j)
+            merge_one(j)
             store(j)
         for s in (4, 5, 6):
-            both((4, 5), s)
-        for j in (4, 5):
-            store(j)
+            both(2, s)
+        store(4)
+        store(5)

@@ -78,9 +78,9 @@ def tile_vclinear_e_kernel(tc, inputs, W_wts_words, W_wts_scales, b_wts, out):
                 out=w_planes[r:P:32].bitcast(I32),
                 in_=W_wts_scales[:, r:16:4, :].rearrange("g Q n -> Q g n").bitcast(I32),
             )
-        load_w(0, 2)
+        load_w(0, 3)
         load_x(1)
-        load_w(2, 5)
+        load_w(3, 5)
         load_w(5, TERMS)
         rows = PIECES * TERMS
         for a in range(GROUP):
@@ -172,6 +172,7 @@ def tile_vclinear_e_kernel(tc, inputs, W_wts_words, W_wts_scales, b_wts, out):
         bias_sb = pair_tiles("bias_sb")
         side = pair_tiles("side")
         total = pair_tiles("total")
+        plain = keep.tile([P, 2, OUTPUTS], F32)
         summed = {}
 
         def half(tiles, j):
@@ -180,6 +181,15 @@ def tile_vclinear_e_kernel(tc, inputs, W_wts_words, W_wts_scales, b_wts, out):
         def start_sum(j):
             summed[j] = acc
             nc.scalar.copy(out=half(acc, j), in_=product(j, 0)[:])
+
+        def start_alone(j, s):
+            summed[j] = acc
+            nc.vector.tensor_scalar(
+                out=half(acc, j), in0=product(j, s)[:], scalar1=basis[:, j, s : s + 1], scalar2=None, op0=ALU.mult
+            )
+
+        def copy_plain(j):
+            nc.scalar.copy(out=plain[:, j, :], in_=product(j, 0)[:])
 
         def add_product(j, s):
             nc.vector.scalar_tensor_tensor(
@@ -231,38 +241,39 @@ def tile_vclinear_e_kernel(tc, inputs, W_wts_words, W_wts_scales, b_wts, out):
         turn(1, 1)
         quantise(1, 1)
         warm_up(WARM_SECOND)
-        start_sum(0)
-        add_product(0, 1)
-        start_sum(1)
-        add_product(1, 1)
+        start_alone(0, 1)
+        start_alone(1, 1)
+        both(0, 2)
+        copy_plain(0)
+        copy_plain(1)
+        both(0, 3)
         turn(2, 2)
         transpose_pieces()
-        both(0, 2)
+        both(0, 4)
         quantise(2, 2)
         scaled(0)
         scaled(1)
-        both(0, 3)
+        nc.gpsimd.tensor_add(out=lin[0][:], in0=lin[0][:], in1=plain[:])
+        both(0, 5)
         bias_term(0)
         bias_term(1)
         add_side(0)
-        both(0, 4)
-        turn(4, 2)
-        turn(6, 2)
-        both(0, 5)
-        quantise(4, 4)
+        both(0, 6)
         start_sum(2)
         start_sum(3)
-        both(0, 6)
         merge(0)
         store_pair(0)
         both(1, 1)
+        turn(4, 2)
+        turn(6, 2)
+        both(1, 2)
+        quantise(4, 4)
         bias_term(2)
         scaled(2)
-        both(1, 2)
+        both(1, 3)
         bias_term(3)
         scaled(3)
         add_side(1)
-        both(1, 3)
         both(1, 4)
         bias_term(4)
         scaled(4)

@@ -70,16 +70,17 @@ def tile_vclinear_e_kernel(tc, inputs, W_wts_words, W_wts_scales, b_wts, out):
                 in_=W_wts_words[first:last].rearrange("g p c -> p g c").bitcast(I32),
             )
 
+        load_x(0)
         with nc.allow_non_contiguous_dma(reason="the treatment is one column of inputs"):
             nc.sync.dma_start(out=t_bf[:], in_=in_rows[:, :, 0:1])
-        load_x(0)
         for r in range(4):
             nc.sync.dma_start(
                 out=w_planes[r:P:32].bitcast(I32),
                 in_=W_wts_scales[:, r:16:4, :].rearrange("g Q n -> Q g n").bitcast(I32),
             )
-        load_w(0, 3)
+        load_w(1, 3)
         load_x(1)
+        load_w(0, 1)
         load_w(3, 5)
         load_w(5, TERMS)
         rows = PIECES * TERMS

@@ -48,7 +48,7 @@ def tile_vclinear_e_kernel(tc, inputs, W_wts_words, W_wts_scales, b_wts, out):
             for i in range(count):
                 nc.tensor.matmul(out=warm_ps[:], lhsT=warm[:, 0:P], rhs=warm[:], start=True, stop=True)
 
-        w_planes = keep.tile([P, TERMS, OUTPUTS], U8, align_bytes=64)
+        w_planes = keep.tile([P, TERMS, OUTPUTS], U8, align_bytes=256)
         nc.vector.memset(w_planes[:].bitcast(I32), 0)
         pieces = keep.tile([P, TILES, PIECES * TERMS], BF16)
         nc.vector.memset(pieces[:].bitcast(I32), 0)
@@ -58,7 +58,7 @@ def tile_vclinear_e_kernel(tc, inputs, W_wts_words, W_wts_scales, b_wts, out):
         nc.vector.memset(basis[:, :, 0:1], 1.0)
 
         x_sb = keep.tile([P, TILES, FEATURES], BF16)
-        w_words = keep.tile([P, TERMS, 2 * OUTPUTS], U8, align_bytes=64)
+        w_words = keep.tile([P, TERMS, 2 * OUTPUTS], U8, align_bytes=256)
         t_bf = keep.tile([P, TILES, 1], BF16)
 
         def load_x(q):
@@ -130,10 +130,10 @@ def tile_vclinear_e_kernel(tc, inputs, W_wts_words, W_wts_scales, b_wts, out):
             nc.scalar.copy(out=piecesT[:], in_=piecesT_ps[:])
 
         x_words = x_sb[:].bitcast(F32)
-        grouped = keep.tile([P, TILES * P * PACK], BF16, align_bytes=64)
+        grouped = keep.tile([P, TILES * P * PACK], BF16, align_bytes=256)
         grouped_words = grouped[:].bitcast(F32).rearrange("p (j b u) -> p j b u", j=TILES, u=2)
-        x_codes = keep.tile([P, TILES * P], U32, align_bytes=64)
-        x_planes = keep.tile([P, TILES * P], U8, align_bytes=64)
+        x_codes = keep.tile([P, TILES * P], U32, align_bytes=256)
+        x_planes = keep.tile([P, TILES * P], U8, align_bytes=256)
 
         def turn(first, count):
             xT = psum.tile([P, count, 2, P], F32, tag="bank", name="xT")

@@ -21,6 +21,7 @@ TERMS = 4 + len(KNOTS)
 TILES = BATCH // P
 WORDS = FEATURES // 2
 PIECES = 4
+BLOCKS = OUTPUTS // P
 GROUP = P // (PIECES * TERMS)
 CHAIN = (1, 2, 3, 4, 5, 6)
 SCALED = 7
@@ -179,6 +180,53 @@ def tile_vclinear_e_kernel(tc, inputs, W_wts_words, W_wts_scales, b_wts, out):
         def half(tiles, j):
             return tiles[j // 2][:, j % 2, :]
 
+        p0T = keep.tile([P, BLOCKS, 2 * P], F32, align_bytes=256)
+        second = keep.tile([P, 2, OUTPUTS], F32)
+
+        def turned_p0(q):
+            cols = slice(2 * P * q, 2 * P * (q + 1))
+            for b in range(0, BLOCKS, 2):
+                bank = psum.tile([P, 2, 2 * P], F32, tag="bank", name="bank")
+                for i in range(2):
+                    o = b + i
+                    nc.tensor.matmul_mx(
+                        out=bank[:, i, :],
+                        lhsT=w_words[:, 0, 2 * P * o : 2 * P * (o + 1)].bitcast(FP4X4),
+                        lhsT_scale=w_planes[:, 0, P * o : P * (o + 1)],
+                        rhs=x_codes[:, cols].bitcast(FP8X4),
+                        rhs_scale=x_planes[:, cols],
+                        start=True,
+                        stop=True,
+                    )
+                nc.scalar.copy(out=p0T[:, b : b + 2, :], in_=bank[:])
+
+        def rest_pair(q):
+            banks = {}
+            for j in (2 * q, 2 * q + 1):
+                bank = psum.tile([P, OUTPUTS], F32, tag="bank", name="bank")
+                nc.tensor.matmul(
+                    out=bank[:], lhsT=piecesT[:, j // GROUP, :], rhs=bias_rhs[:, j % GROUP, :], start=True, stop=False
+                )
+                banks[j] = bank
+            for j in (2 * q, 2 * q + 1):
+                for o in range(BLOCKS):
+                    nc.tensor.matmul(
+                        out=banks[j][:, P * o : P * (o + 1)],
+                        lhsT=p0T[:, o, P * (j % 2) : P * (j % 2 + 1)],
+                        rhs=ident_f32[:],
+                        is_transpose=True,
+                        start=False,
+                        stop=o == BLOCKS - 1,
+                    )
+            for j in (2 * q, 2 * q + 1):
+                summed[j] = acc
+                nc.scalar.copy(out=half(acc, j), in_=banks[j][:])
+
+        def scale_six(j):
+            nc.scalar.activation(
+                out=second[:, j % 2, :], in_=product(j, 6)[:], func=ACT.Copy, scale=basis[:, j, 6:7]
+            )
+
         def start_sum(j):
             summed[j] = acc
             nc.scalar.copy(out=half(acc, j), in_=product(j, 0)[:])
@@ -224,6 +272,10 @@ def tile_vclinear_e_kernel(tc, inputs, W_wts_words, W_wts_scales, b_wts, out):
 
         def merge_one(j):
             nc.gpsimd.tensor_add(out=half(total, j), in0=half(acc, j), in1=half(side, j))
+            summed[j] = total
+
+        def finish(j):
+            nc.gpsimd.tensor_add(out=half(total, j), in0=half(acc, j), in1=half(lin, j))
             summed[j] = total
 
         def store(j):
@@ -288,24 +340,25 @@ def tile_vclinear_e_kernel(tc, inputs, W_wts_words, W_wts_scales, b_wts, out):
         merge(1)
         store_pair(1)
         both(2, 1)
-        start_sum(6)
+        turned_p0(3)
         both(2, 2)
-        start_sum(7)
         both(2, 3)
         merge(2)
-        bias_term(6)
-        scaled(6)
+        rest_pair(3)
         both(3, 1)
-        bias_term(7)
-        both(3, 2)
+        scaled(6)
         scaled(7)
-        add_side(3)
-        for s in (3, 4, 5, 6):
+        both(3, 2)
+        scale_six(6)
+        scale_six(7)
+        nc.gpsimd.tensor_add(out=lin[3][:], in0=lin[3][:], in1=second[:])
+        for s in (3, 4, 5):
             both(3, s)
-        for j in (6, 7):
-            merge_one(j)
-            store(j)
+        finish(6)
+        store(6)
+        finish(7)
         for s in (4, 5, 6):
             both(2, s)
         store(4)
         store(5)
+        store(7)

@@ -79,8 +79,9 @@ def tile_vclinear_e_kernel(tc, inputs, W_wts_words, W_wts_scales, b_wts, out):
                 out=w_planes[r:P:32].bitcast(I32),
                 in_=W_wts_scales[:, r:16:4, :].rearrange("g Q n -> Q g n").bitcast(I32),
             )
-        load_w(1, 3)
+        load_w(1, 2)
         load_x(1)
+        load_w(2, 3)
         load_w(0, 1)
         load_w(3, 5)
         load_w(5, TERMS)
@@ -200,27 +201,23 @@ def tile_vclinear_e_kernel(tc, inputs, W_wts_words, W_wts_scales, b_wts, out):
                     )
                 nc.scalar.copy(out=p0T[:, b : b + 2, :], in_=bank[:])
 
-        def rest_pair(q):
-            banks = {}
-            for j in (2 * q, 2 * q + 1):
-                bank = psum.tile([P, OUTPUTS], F32, tag="bank", name="bank")
+        def rest(j, also=None):
+            bank = psum.tile([P, OUTPUTS], F32, tag="bank", name="bank")
+            nc.tensor.matmul(
+                out=bank[:], lhsT=piecesT[:, j // GROUP, :], rhs=bias_rhs[:, j % GROUP, :], start=True, stop=False
+            )
+            for o in range(BLOCKS):
                 nc.tensor.matmul(
-                    out=bank[:], lhsT=piecesT[:, j // GROUP, :], rhs=bias_rhs[:, j % GROUP, :], start=True, stop=False
+                    out=bank[:, P * o : P * (o + 1)],
+                    lhsT=p0T[:, o, P * (j % 2) : P * (j % 2 + 1)],
+                    rhs=ident_f32[:],
+                    is_transpose=True,
+                    start=False,
+                    stop=o == BLOCKS - 1 and also is None,
                 )
-                banks[j] = bank
-            for j in (2 * q, 2 * q + 1):
-                for o in range(BLOCKS):
-                    nc.tensor.matmul(
-                        out=banks[j][:, P * o : P * (o + 1)],
-                        lhsT=p0T[:, o, P * (j % 2) : P * (j % 2 + 1)],
-                        rhs=ident_f32[:],
-                        is_transpose=True,
-                        start=False,
-                        stop=o == BLOCKS - 1,
-                    )
-            for j in (2 * q, 2 * q + 1):
-                summed[j] = acc
-                nc.scalar.copy(out=half(acc, j), in_=banks[j][:])
+            if also is not None:
+                nc.tensor.matmul(out=bank[:], lhsT=ident_f32[:], rhs=also, start=False, stop=True)
+            nc.scalar.copy(out=half(bias_sb, j), in_=bank[:])
 
         def scale_six(j):
             nc.scalar.activation(
@@ -250,6 +247,17 @@ def tile_vclinear_e_kernel(tc, inputs, W_wts_words, W_wts_scales, b_wts, out):
                 op1=ALU.add,
             )
 
+        def begin(j, s, base):
+            summed[j] = acc
+            nc.vector.scalar_tensor_tensor(
+                out=half(acc, j),
+                in0=product(j, s)[:],
+                scalar=basis[:, j, s : s + 1],
+                in1=half(base, j),
+                op0=ALU.mult,
+                op1=ALU.add,
+            )
+
         def scaled(j):
             nc.scalar.activation(
                 out=half(lin, j), in_=product(j, SCALED)[:], func=ACT.Copy, scale=basis[:, j, SCALED : SCALED + 1]
@@ -274,8 +282,8 @@ def tile_vclinear_e_kernel(tc, inputs, W_wts_words, W_wts_scales, b_wts, out):
             nc.gpsimd.tensor_add(out=half(total, j), in0=half(acc, j), in1=half(side, j))
             summed[j] = total
 
-        def finish(j):
-            nc.gpsimd.tensor_add(out=half(total, j), in0=half(acc, j), in1=half(lin, j))
+        def finish(j, part):
+            nc.gpsimd.tensor_add(out=half(total, j), in0=half(acc, j), in1=half(part, j))
             summed[j] = total
 
         def store(j):
@@ -344,19 +352,22 @@ def tile_vclinear_e_kernel(tc, inputs, W_wts_words, W_wts_scales, b_wts, out):
         both(2, 2)
         both(2, 3)
         merge(2)
-        rest_pair(3)
-        both(3, 1)
-        scaled(6)
+        rest(6)
         scaled(7)
+        begin(6, 1, bias_sb)
+        begin(7, 1, lin)
+        scaled(6)
+        scale_six(7)
         both(3, 2)
         scale_six(6)
-        scale_six(7)
-        nc.gpsimd.tensor_add(out=lin[3][:], in0=lin[3][:], in1=second[:])
-        for s in (3, 4, 5):
-            both(3, s)
-        finish(6)
+        nc.gpsimd.tensor_add(out=half(lin, 6), in0=half(lin, 6), in1=second[:, 0, :])
+        both(3, 3)
+        both(3, 4)
+        both(3, 5)
+        rest(7, second[:, 1, :])
+        finish(6, lin)
         store(6)
-        finish(7)
+        finish(7, bias_sb)
         for s in (4, 5, 6):
             both(2, s)
         store(4)

@@ -183,6 +183,7 @@ def tile_vclinear_e_kernel(tc, inputs, W_wts_words, W_wts_scales, b_wts, out):
 
         p0T = keep.tile([P, BLOCKS, 2 * P], F32, align_bytes=256)
         second = keep.tile([P, 2, OUTPUTS], F32)
+        third = keep.tile([P, OUTPUTS], F32)
 
         def turned_p0(q):
             cols = slice(2 * P * q, 2 * P * (q + 1))
@@ -201,7 +202,9 @@ def tile_vclinear_e_kernel(tc, inputs, W_wts_words, W_wts_scales, b_wts, out):
                     )
                 nc.scalar.copy(out=p0T[:, b : b + 2, :], in_=bank[:])
 
-        def rest(j, also=None):
+        rest_banks = {}
+
+        def open_rest(j):
             bank = psum.tile([P, OUTPUTS], F32, tag="bank", name="bank")
             nc.tensor.matmul(
                 out=bank[:], lhsT=piecesT[:, j // GROUP, :], rhs=bias_rhs[:, j % GROUP, :], start=True, stop=False
@@ -213,11 +216,21 @@ def tile_vclinear_e_kernel(tc, inputs, W_wts_words, W_wts_scales, b_wts, out):
                     rhs=ident_f32[:],
                     is_transpose=True,
                     start=False,
-                    stop=o == BLOCKS - 1 and also is None,
+                    stop=False,
                 )
-            if also is not None:
-                nc.tensor.matmul(out=bank[:], lhsT=ident_f32[:], rhs=also, start=False, stop=True)
+            rest_banks[j] = bank
+
+        def close_rest(j, part):
+            bank = rest_banks[j]
+            nc.tensor.matmul(out=bank[:], lhsT=ident_f32[:], rhs=part, start=False, stop=True)
             nc.scalar.copy(out=half(bias_sb, j), in_=bank[:])
+
+        def rest(j, part):
+            open_rest(j)
+            close_rest(j, part)
+
+        def scale_five(j):
+            nc.scalar.activation(out=third[:], in_=product(j, 5)[:], func=ACT.Copy, scale=basis[:, j, 5:6])
 
         def scale_six(j):
             nc.scalar.activation(
@@ -350,26 +363,30 @@ def tile_vclinear_e_kernel(tc, inputs, W_wts_words, W_wts_scales, b_wts, out):
         both(2, 1)
         turned_p0(3)
         both(2, 2)
-        both(2, 3)
-        merge(2)
-        rest(6)
-        scaled(7)
-        begin(6, 1, bias_sb)
-        begin(7, 1, lin)
         scaled(6)
+        scaled(7)
+        both(2, 3)
+        both(2, 4)
+        merge(2)
+        scale_five(6)
+        begin(6, 1, lin)
+        begin(7, 1, lin)
+        scale_six(6)
         scale_six(7)
         both(3, 2)
-        scale_six(6)
-        nc.gpsimd.tensor_add(out=half(lin, 6), in0=half(lin, 6), in1=second[:, 0, :])
         both(3, 3)
+        rest(6, third[:])
+        nc.gpsimd.tensor_add(out=half(bias_sb, 6), in0=half(bias_sb, 6), in1=second[:, 0, :])
         both(3, 4)
-        both(3, 5)
-        rest(7, second[:, 1, :])
-        finish(6, lin)
+        add_product(4, 5)
+        add_product(7, 5)
+        open_rest(7)
+        add_product(5, 5)
+        close_rest(7, second[:, 1, :])
+        finish(6, bias_sb)
         store(6)
         finish(7, bias_sb)
-        for s in (4, 5, 6):
-            both(2, s)
+        both(2, 6)
         store(4)
         store(5)
         store(7)

from contextlib import ExitStack

import concourse.mybir as mybir
from concourse.masks import make_identity

F32 = mybir.dt.float32
BF16 = mybir.dt.bfloat16
I32 = mybir.dt.int32
U8 = mybir.dt.uint8
U32 = mybir.dt.uint32
FP8X4 = mybir.dt.float8_e4m3fn_x4
FP4X4 = mybir.dt.float4_e2m1fn_x4
ALU = mybir.AluOpType
ACT = mybir.ActivationFunctionType

P = 128
PACK = 4
BATCH, FEATURES, OUTPUTS = 1024, 512, 512
KNOTS = (0.2, 0.4, 0.6, 0.8)
TERMS = 4 + len(KNOTS)
TILES = BATCH // P
WORDS = FEATURES // 2
PIECES = 4
BLOCKS = OUTPUTS // P
GROUP = P // (PIECES * TERMS)
CHAIN = (1, 2, 3, 4, 5, 6)
SCALED = 7
WARM_FIRST = 4
WARM_SECOND = 3

FLOPS = 2 * BATCH * FEATURES * OUTPUTS * TERMS + 2 * BATCH * TERMS * OUTPUTS


def tile_vclinear_e_kernel(tc, inputs, W_wts_words, W_wts_scales, b_wts, out):
    nc = tc.nc
    in_rows = inputs.rearrange("(p j) c -> p j c", j=TILES)
    out_rows = out.rearrange("(p j) o -> p j o", j=TILES)

    with ExitStack() as stack:
        keep = stack.enter_context(tc.tile_pool(name="keep", bufs=1))
        psum = stack.enter_context(tc.psum_pool(name="psum", bufs=8))
        stack.enter_context(tc.manual_schedule())

        warm = keep.tile([P, OUTPUTS], BF16)
        nc.gpsimd.memset(warm[:], 0.0)
        warm_ps = psum.tile([P, OUTPUTS], F32, tag="bank")

        def warm_up(count):
            for i in range(count):
                nc.tensor.matmul(out=warm_ps[:], lhsT=warm[:, 0:P], rhs=warm[:], start=True, stop=True)

        w_planes = keep.tile([P, TERMS, OUTPUTS], U8, align_bytes=256)
        nc.vector.memset(w_planes[:].bitcast(I32), 0)
        pieces = keep.tile([P, TILES, PIECES * TERMS], BF16)
        nc.vector.memset(pieces[:].bitcast(I32), 0)
        bias_rhs = keep.tile([P, GROUP, OUTPUTS], BF16)
        nc.vector.memset(bias_rhs[:].bitcast(I32), 0)
        basis = keep.tile([P, TILES, TERMS], F32)
        nc.vector.memset(basis[:, :, 0:1], 1.0)

        x_sb = keep.tile([P, TILES, FEATURES], BF16)
        w_words = keep.tile([P, TERMS, 2 * OUTPUTS], U8, align_bytes=256)
        t_bf = keep.tile([P, TILES, 1], BF16)

        def load_x(q):
            nc.sync.dma_start(out=x_sb[:, 2 * q : 2 * q + 2, :], in_=in_rows[:, 2 * q : 2 * q + 2, 1:])

        def load_w(first, last):
            nc.sync.dma_start(
                out=w_words[:, first:last, :].bitcast(I32),
                in_=W_wts_words[first:last].rearrange("g p c -> p g c").bitcast(I32),
            )

        load_x(0)
        with nc.allow_non_contiguous_dma(reason="the treatment is one column of inputs"):
            nc.sync.dma_start(out=t_bf[:], in_=in_rows[:, :, 0:1])
        for r in range(4):
            nc.sync.dma_start(
                out=w_planes[r:P:32].bitcast(I32),
                in_=W_wts_scales[:, r:16:4, :].rearrange("g Q n -> Q g n").bitcast(I32),
            )
        load_w(1, 2)
        load_x(1)
        load_w(2, 3)
        load_w(0, 1)
        load_w(3, 5)
        load_w(5, TERMS)
        rows = PIECES * TERMS
        for a in range(GROUP):
            nc.sync.dma_start(
                out=bias_rhs[rows * a : rows * (a + 1), a, :],
                in_=b_wts.unsqueeze(0).to_broadcast([PIECES, TERMS, OUTPUTS]),
            )
        load_x(2)
        load_x(3)

        ident_f32 = keep.tile([P, P], F32)
        make_identity(nc, ident_f32[:])
        ident_bf = keep.tile([P, P], BF16)
        nc.scalar.copy(out=ident_bf[:], in_=ident_f32[:])

        hinge = keep.tile([P, TILES, len(KNOTS)], F32)
        hinge_sq = keep.tile([P, TILES, len(KNOTS)], F32)
        nc.vector.tensor_copy(out=basis[:, :, 1:2], in_=t_bf[:])
        for c, knot in enumerate(KNOTS):
            nc.vector.tensor_scalar(
                out=hinge[:, :, c : c + 1], in0=t_bf[:], scalar1=knot, scalar2=0.0, op0=ALU.subtract, op1=ALU.max
            )
        nc.vector.tensor_mul(out=basis[:, :, 2:3], in0=t_bf[:], in1=t_bf[:])
        nc.vector.tensor_mul(out=hinge_sq[:], in0=hinge[:], in1=hinge[:])
        nc.vector.tensor_mul(out=basis[:, :, 3:4], in0=basis[:, :, 2:3], in1=basis[:, :, 1:2])
        nc.vector.tensor_mul(out=basis[:, :, 4:], in0=hinge_sq[:], in1=hinge[:])

        rest = basis
        for c in range(3):
            piece = pieces[:, :, TERMS * c : TERMS * (c + 1)]
            nc.gpsimd.tensor_copy(out=piece, in_=rest[:])
            if c < 2:
                smaller = keep.tile([P, TILES, TERMS], F32, name="rest%d" % c)
                nc.gpsimd.tensor_sub(out=smaller[:], in0=rest[:], in1=piece)
                rest = smaller
        piecesT = keep.tile([P, TILES // GROUP, P], BF16)

        def transpose_pieces():
            piecesT_ps = psum.tile([P, TILES // GROUP, P], BF16, tag="bank")
            for h in range(TILES // GROUP):
                nc.tensor.transpose(
                    piecesT_ps[:, h, :],
                    pieces[:, GROUP * h : GROUP * (h + 1), :].rearrange("p j k -> p (j k)"),
                    ident_bf[:],
                )
            nc.scalar.copy(out=piecesT[:], in_=piecesT_ps[:])

        x_words = x_sb[:].bitcast(F32)
        grouped = keep.tile([P, TILES * P * PACK], BF16, align_bytes=256)
        grouped_words = grouped[:].bitcast(F32).rearrange("p (j b u) -> p j b u", j=TILES, u=2)
        x_codes = keep.tile([P, TILES * P], U32, align_bytes=256)
        x_planes = keep.tile([P, TILES * P], U8, align_bytes=256)

        def turn(first, count):
            xT = psum.tile([P, count, 2, P], F32, tag="bank", name="xT")
            for i in range(count):
                for u in range(2):
                    nc.tensor.transpose(xT[:, i, u, :], x_words[:, first + i, u:WORDS:2], ident_f32[:])
            nc.scalar.copy(
                out=grouped_words[:, first : first + count], in_=xT[:].rearrange("p i u b -> p i b u")
            )

        def quantise(first, count):
            cols = slice(P * first, P * (first + count))
            nc.vector.quantize_mx(
                out=x_codes[:, cols].bitcast(FP8X4),
                scales=x_planes[:, cols],
                in_=grouped[:, P * PACK * first : P * PACK * (first + count)],
            )

        def product(j, s):
            bank = psum.tile([P, OUTPUTS], F32, tag="bank", name="bank")
            nc.tensor.matmul_mx(
                out=bank[:],
                lhsT=x_codes[:, P * j : P * (j + 1)].bitcast(FP8X4),
                lhsT_scale=x_planes[:, P * j : P * (j + 1)],
                rhs=w_words[:, s, :].bitcast(FP4X4),
                rhs_scale=w_planes[:, s, :],
                start=True,
                stop=True,
            )
            return bank

        def pair_tiles(name):
            return [keep.tile([P, 2, OUTPUTS], F32, name="%s%d" % (name, q)) for q in range(TILES // 2)]

        acc = pair_tiles("acc")
        lin = pair_tiles("lin")
        bias_sb = pair_tiles("bias_sb")
        side = pair_tiles("side")
        total = pair_tiles("total")
        plain = keep.tile([P, 2, OUTPUTS], F32)
        summed = {}

        def half(tiles, j):
            return tiles[j // 2][:, j % 2, :]

        p0T = keep.tile([P, BLOCKS, 2 * P], F32, align_bytes=256)
        second = keep.tile([P, 2, OUTPUTS], F32)
        third = keep.tile([P, OUTPUTS], F32)

        def turned_p0(q):
            cols = slice(2 * P * q, 2 * P * (q + 1))
            for b in range(0, BLOCKS, 2):
                bank = psum.tile([P, 2, 2 * P], F32, tag="bank", name="bank")
                for i in range(2):
                    o = b + i
                    nc.tensor.matmul_mx(
                        out=bank[:, i, :],
                        lhsT=w_words[:, 0, 2 * P * o : 2 * P * (o + 1)].bitcast(FP4X4),
                        lhsT_scale=w_planes[:, 0, P * o : P * (o + 1)],
                        rhs=x_codes[:, cols].bitcast(FP8X4),
                        rhs_scale=x_planes[:, cols],
                        start=True,
                        stop=True,
                    )
                nc.scalar.copy(out=p0T[:, b : b + 2, :], in_=bank[:])

        rest_banks = {}

        def open_rest(j):
            bank = psum.tile([P, OUTPUTS], F32, tag="bank", name="bank")
            nc.tensor.matmul(
                out=bank[:], lhsT=piecesT[:, j // GROUP, :], rhs=bias_rhs[:, j % GROUP, :], start=True, stop=False
            )
            for o in range(BLOCKS):
                nc.tensor.matmul(
                    out=bank[:, P * o : P * (o + 1)],
                    lhsT=p0T[:, o, P * (j % 2) : P * (j % 2 + 1)],
                    rhs=ident_f32[:],
                    is_transpose=True,
                    start=False,
                    stop=False,
                )
            rest_banks[j] = bank

        def close_rest(j, part):
            bank = rest_banks[j]
            nc.tensor.matmul(out=bank[:], lhsT=ident_f32[:], rhs=part, start=False, stop=True)
            nc.scalar.copy(out=half(bias_sb, j), in_=bank[:])

        def rest(j, part):
            open_rest(j)
            close_rest(j, part)

        def scale_five(j):
            nc.scalar.activation(out=third[:], in_=product(j, 5)[:], func=ACT.Copy, scale=basis[:, j, 5:6])

        def scale_six(j):
            nc.scalar.activation(
                out=second[:, j % 2, :], in_=product(j, 6)[:], func=ACT.Copy, scale=basis[:, j, 6:7]
            )

        def start_sum(j):
            summed[j] = acc
            nc.scalar.copy(out=half(acc, j), in_=product(j, 0)[:])

        def start_alone(j, s):
            summed[j] = acc
            nc.vector.tensor_scalar(
                out=half(acc, j), in0=product(j, s)[:], scalar1=basis[:, j, s : s + 1], scalar2=None, op0=ALU.mult
            )

        def copy_plain(j):
            nc.scalar.copy(out=plain[:, j, :], in_=product(j, 0)[:])

        def add_product(j, s):
            nc.vector.scalar_tensor_tensor(
                out=half(summed[j], j),
                in0=product(j, s)[:],
                scalar=basis[:, j, s : s + 1],
                in1=half(summed[j], j),
                op0=ALU.mult,
                op1=ALU.add,
            )

        def begin(j, s, base):
            summed[j] = acc
            nc.vector.scalar_tensor_tensor(
                out=half(acc, j),
                in0=product(j, s)[:],
                scalar=basis[:, j, s : s + 1],
                in1=half(base, j),
                op0=ALU.mult,
                op1=ALU.add,
            )

        def scaled(j):
            nc.scalar.activation(
                out=half(lin, j), in_=product(j, SCALED)[:], func=ACT.Copy, scale=basis[:, j, SCALED : SCALED + 1]
            )

        def bias_term(j):
            bias_ps = psum.tile([P, OUTPUTS], F32, tag="bank")
            nc.tensor.matmul(
                out=bias_ps[:], lhsT=piecesT[:, j // GROUP, :], rhs=bias_rhs[:, j % GROUP, :], start=True, stop=True
            )
            nc.scalar.copy(out=half(bias_sb, j), in_=bias_ps[:])

        def add_side(q):
            nc.gpsimd.tensor_add(out=side[q][:], in0=bias_sb[q][:], in1=lin[q][:])

        def merge(q):
            nc.gpsimd.tensor_add(out=total[q][:], in0=acc[q][:], in1=side[q][:])
            summed[2 * q] = total
            summed[2 * q + 1] = total

        def merge_one(j):
            nc.gpsimd.tensor_add(out=half(total, j), in0=half(acc, j), in1=half(side, j))
            summed[j] = total

        def finish(j, part):
            nc.gpsimd.tensor_add(out=half(total, j), in0=half(acc, j), in1=half(part, j))
            summed[j] = total

        def store(j):
            nc.sync.dma_start(out=out_rows[:, j, :], in_=half(summed[j], j))

        def store_pair(q):
            nc.sync.dma_start(out=out_rows[:, 2 * q : 2 * q + 2, :], in_=total[q][:])

        def both(q, s):
            for j in (2 * q, 2 * q + 1):
                add_product(j, s)

        warm_up(WARM_FIRST)
        turn(0, 1)
        quantise(0, 1)
        turn(1, 1)
        quantise(1, 1)
        warm_up(WARM_SECOND)
        start_alone(0, 1)
        start_alone(1, 1)
        both(0, 2)
        copy_plain(0)
        copy_plain(1)
        both(0, 3)
        turn(2, 2)
        transpose_pieces()
        both(0, 4)
        quantise(2, 2)
        scaled(0)
        scaled(1)
        nc.gpsimd.tensor_add(out=lin[0][:], in0=lin[0][:], in1=plain[:])
        both(0, 5)
        bias_term(0)
        bias_term(1)
        add_side(0)
        both(0, 6)
        start_sum(2)
        start_sum(3)
        merge(0)
        store_pair(0)
        both(1, 1)
        turn(4, 2)
        turn(6, 2)
        both(1, 2)
        quantise(4, 4)
        bias_term(2)
        scaled(2)
        both(1, 3)
        bias_term(3)
        scaled(3)
        add_side(1)
        both(1, 4)
        bias_term(4)
        scaled(4)
        both(1, 5)
        start_sum(4)
        start_sum(5)
        both(1, 6)
        bias_term(5)
        scaled(5)
        add_side(2)
        merge(1)
        store_pair(1)
        both(2, 1)
        turned_p0(3)
        both(2, 2)
        scaled(6)
        scaled(7)
        both(2, 3)
        both(2, 4)
        merge(2)
        scale_five(6)
        begin(6, 1, lin)
        begin(7, 1, lin)
        scale_six(6)
        scale_six(7)
        both(3, 2)
        both(3, 3)
        rest(6, third[:])
        nc.gpsimd.tensor_add(out=half(bias_sb, 6), in0=half(bias_sb, 6), in1=second[:, 0, :])
        both(3, 4)
        add_product(4, 5)
        add_product(7, 5)
        open_rest(7)
        add_product(5, 5)
        close_rest(7, second[:, 1, :])
        finish(6, bias_sb)
        store(6)
        finish(7, bias_sb)
        both(2, 6)
        store(4)
        store(5)
        store(7)
